import numpy as np
import ml_dtypes


def mxq(x, axis, fmt="e4m3"):
    dtype, down = {"e4m3": (ml_dtypes.float8_e4m3fn, 7), "e5m2": (ml_dtypes.float8_e5m2, 14)}[fmt]
    v = np.moveaxis(np.asarray(x, np.float32).astype(ml_dtypes.bfloat16).astype(np.float64), axis, -1)
    blocks = v.reshape(v.shape[:-1] + (-1, 32))
    amax = np.abs(blocks).max(-1, keepdims=True)
    byte = np.maximum(np.where(amax > 0, np.frexp(amax)[1] - 1 + 127, 0) - down, 1)
    scale = np.exp2(byte - 127.0)
    codes = (blocks / scale).astype(np.float32).astype(dtype).astype(np.float64)
    return np.moveaxis((codes * scale).reshape(v.shape), -1, axis)


WIDE = False


def mx_kscale(k):
    if not WIDE:
        return np.ones(k)
    levels = np.array([18, -18])
    if k % 512:
        return np.exp2(np.random.permutation(np.resize(levels, k // 32))).repeat(32)
    a = np.empty((k // 512, 16))
    for p in range(k // 512):
        a[p, :8] = np.random.permutation(np.resize(levels, 8))
        for g in range(8):
            far = levels[np.abs(levels - a[p, g]) >= 10]
            a[p, g + 8] = far[np.random.randint(len(far))]
    return np.exp2(a.ravel()).repeat(32)


BF16 = ml_dtypes.bfloat16


def bf(x):
    return np.asarray(x, np.float32).astype(BF16)


def f64(x):
    return np.asarray(x).astype(np.float64)


B, I, H = 1024, 512, 1024
C = I + H


def hard_sigmoid(v):
    return np.clip(v / 6.0 + 0.5, 0.0, 1.0)


def hard_tanh(v):
    return np.clip(v, -1.0, 1.0)


def clear_of_edges(y, b, edge):
    b = f64(b)
    for _ in range(50):
        near = (np.abs(np.abs(y + b) - edge) < 2e-4).any(axis=0)
        if not near.any():
            break
        b = np.where(near, f64(bf(b + 0.0625)), b)
    return bf(b)


def setup_inputs():
    s = mx_kscale(B)[:, None]
    u = mx_kscale(H)
    v = mx_kscale(H)
    n = 1.0 / np.max(s) ** 2
    x0 = bf(np.random.standard_normal((B, I)))
    h0 = bf(np.random.standard_normal((B, H)))
    wz0 = bf(np.random.standard_normal((H, C)) * 2.5 / np.sqrt(C))
    b_z = bf(np.random.standard_normal(H) * 1.0)
    wr0 = bf(np.random.standard_normal((H, C)) * 2.5 / np.sqrt(C))
    b_r = bf(np.random.standard_normal(H) * 1.0)
    wh0 = bf(np.random.standard_normal((H, C)) * 1.2 / np.sqrt(C))
    b_h = bf(np.random.standard_normal(H) * 0.5)
    g = bf(4.0 * np.random.standard_normal((B, H)) * np.exp2(np.random.randint(-6, 1, (B, 1))) * u * n)
    ih = np.concatenate([f64(x0), f64(h0)], axis=1)
    y_z = ih @ f64(wz0).T
    b_z = clear_of_edges(y_z, b_z, 3.0)
    a_z = y_z + f64(b_z)
    y_r = ih @ f64(wr0).T
    b_r = clear_of_edges(y_r, b_r, 3.0)
    a_r = y_r + f64(b_r)
    irh = np.concatenate([f64(x0), hard_sigmoid(a_r) * f64(h0)], axis=1)
    y_h = irh @ f64(wh0).T
    b_h = clear_of_edges(y_h, b_h, 1.0)
    a_h = y_h + f64(b_h)
    vc = np.concatenate([np.ones(I), v])
    return {"inputs": bf(f64(x0) / s / n),
            "h_prev": bf(f64(h0) * s),
            "W_z": bf(f64(wz0) / u[:, None]),
            "b_z": b_z,
            "W_r": bf(f64(wr0) / v[:, None]),
            "b_r": b_r,
            "W_h": bf(f64(wh0) * vc / u[:, None]),
            "b_h": b_h,
            "a_z": np.asarray(a_z, np.float32),
            "a_r": np.asarray(a_r, np.float32),
            "a_h": np.asarray(a_h, np.float32),
            "grad_out": g}


def reference(inputs, h_prev, W_z, b_z, W_r, b_r, W_h, b_h, a_z, a_r, a_h, grad_out):
    h, g = f64(h_prev), f64(grad_out)
    az, ar, ah = f64(a_z), f64(a_r), f64(a_h)
    z, r, h_tilde = hard_sigmoid(az), hard_sigmoid(ar), hard_tanh(ah)
    dz2 = g * (1.0 - z) * np.where(np.abs(ah) < 1.0, 1.0, 0.0)
    d_rh = mxq(dz2, 1, "e5m2") @ mxq(f64(W_h)[:, I:], 0, "e4m3")
    da_r = d_rh * h * np.where(np.abs(ar) < 3.0, 1.0 / 6.0, 0.0)
    da_z = g * (h - h_tilde) * np.where(np.abs(az) < 3.0, 1.0 / 6.0, 0.0)
    dgates = np.concatenate([da_z, da_r], axis=1)
    w_gates = np.concatenate([f64(W_z)[:, I:], f64(W_r)[:, I:]], axis=0)
    dh_prev = (mxq(dgates, 1, "e5m2") @ mxq(w_gates, 0, "e4m3")) + g * z + d_rh * r
    ih = np.concatenate([f64(inputs), h], axis=1)
    dW_r = mxq(da_r, 0, "e5m2").T @ mxq(ih, 0, "e4m3")
    return dh_prev, dW_r

from contextlib import ExitStack
import math

import concourse.mybir as mybir
from concourse.masks import make_identity

F32 = mybir.dt.float32
BF16 = mybir.dt.bfloat16
U32 = mybir.dt.uint32
U8 = mybir.dt.uint8
E4M3X4 = mybir.dt.float8_e4m3fn_x4
E5M2X4 = mybir.dt.float8_e5m2_x4
ACT = mybir.ActivationFunctionType
ALU = mybir.AluOpType

B, I, H = 1024, 512, 1024
C = I + H
FLOPS = 2 * B * H * H + 2 * B * 2 * H * H + 2 * H * B * C
BYTES = 2 * (B * I + B * H + 3 * H * H + B * H) + 4 * 3 * B * H + 4 * (B * H + H * C)

P = 128
PACK = 4
NB = 512
TILES = 8
KP = 2

SIXTH = 1.0 / 6.0
EDGE = 1.0 + 2.0 ** -8
ROOT_1 = math.sqrt(EDGE) * (1.0 + 2.0 ** -22)
ROOT_3 = ROOT_1 / 3.0

AZB, B2K = 3, 6


def il_cut(key, c0, c1, step=256):
    return [("il", key, c, min(c + step, c1)) for c in range(c0, c1, step)]


def in_cut(g):
    return [("ilin", g, c, c + 256) for c in (0, 256)]


LOADS = {(1,): [("load", ("h", 1))], (4,): [("load", "in")], (5,): [("load", ("z", 0))], (7,): [("load", ("z", 1))], ("u", 1): [("load", ("r", 0))], ("u", 3): [("load", ("r", 1))]}
V1 = {
    (0, 0): [("new", ("h", 0))] + il_cut(("h", 0), 0, 512, 512),
    (0, 1): il_cut(("h", 0), 512, 1024, 512),
    (1, 0): [("qw", ("h", 0))],
    (2, 0): [("new", ("h", 1))] + il_cut(("h", 1), 0, 512, 512),
    (3, 0): il_cut(("h", 1), 512, 1024, 512), (4, 0): [("qw", ("h", 1))],
    (6, 0): [("qin", 0), ("qin", 1)],
    (7, 1): [("qh", 0, 0, 1024)],
    (8, 1): [("new", ("z", 0))] + il_cut(("z", 0), 0, 1024, 512),
}
S1 = {
    (5, 0): [("new", "in")] + in_cut(0), (5, 1): in_cut(1),
    (6, 0): [("new", "h0")] + il_cut("h0", 0, 256), (6, 1): il_cut("h0", 256, 512),
    (7, 0): il_cut("h0", 512, 1024),
    (8, 0): [("new", "h1")] + il_cut("h1", 0, 512),
}
V2 = {
    (0, 2): [("qw", ("z", 0)), ("qh", 1, 0, 1024)],
    (2, 2): [("new", ("z", 1))] + il_cut(("z", 1), 0, 1024, 512) + [("qw", ("z", 1)), ("qd", 0, 0, 0, 512)],
    (4, 0): il_cut(("d", 1, 0), 0, 256),
    (4, 2): [("qd", 1, 0, 0, 256), ("qd", 1, 0, 256, 512)],
    (4, 1): [("qw", ("r", 0))],
    (5, 2): [("qw", ("r", 1)), ("out0", 0), ("out0", 1)],
    (6, 0): [("out", 0), ("out", 1)],
    (6, 2): [("out0", 2), ("out0", 3)],
    (7, 0): [("out", 2), ("out", 3)],
    (7, 2): [("qd", 0, 1, 0, 512), ("out0", 4), ("out0", 5)],
    (8, 0): il_cut(("d", 1, 1), 0, 256) + [("out", 4), ("out", 5), ("qd", 1, 1, 0, 256)],
    (8, 2): [("qd", 1, 1, 256, 512), ("out0", 6), ("out", 6), ("out0", 7), ("out", 7)],
}
S2 = {
    (0, 0): il_cut("h1", 512, 1024),
    (2, 1): [("new", ("d", 0, 0))] + il_cut(("d", 0, 0), 0, 512),
    (3, 0): [("new", ("r", 0))] + il_cut(("r", 0), 0, 512), (3, 1): il_cut(("r", 0), 512, 1024),
    (4, 0): [("new", ("d", 1, 0))] + il_cut(("d", 1, 0), 256, 512),
    (4, 1): [("new", ("r", 1))] + il_cut(("r", 1), 0, 512),
    (5, 0): il_cut(("r", 1), 512, 1024),
    (5, 1): [("x", 0, 4)],
    (6, 0): [("new", ("d", 0, 1))] + il_cut(("d", 0, 1), 0, 256), (6, 1): il_cut(("d", 0, 1), 256, 512) + [("x", 4, 8)],
    (7, 1): [("x", 8, 12)],
    (8, 0): [("new", ("d", 1, 1))] + il_cut(("d", 1, 1), 256, 512),
    (8, 2): [("x", 12, 24)],
}


def tile_grucell_v_kernel(
    tc, inputs, h_prev, W_z, b_z, W_r, b_r, W_h, b_h, a_z, a_r, a_h, grad_out, out_0, out_1
):
    nc = tc.nc
    V, S, G, PE, Q = nc.vector, nc.scalar, nc.gpsimd, nc.tensor, nc.sync

    def tokens(x):
        return x.rearrange("(g p j) w -> p g j w", g=KP, j=PACK)

    az_h, ar_h, ah_h = tokens(a_z), tokens(a_r), tokens(a_h)
    g_h, h_h, in_h, o0_h = tokens(grad_out), tokens(h_prev), tokens(inputs), tokens(out_0)
    w_h = {n: w[:, I:].rearrange("(k p j) c -> p k j c", k=KP, j=PACK) for n, w in (("h", W_h), ("z", W_z), ("r", W_r))}

    with ExitStack() as ctx:
        pool = ctx.enter_context(tc.tile_pool(name="sb", bufs=1))
        psum = ctx.enter_context(tc.psum_pool(name="ps", bufs=1))

        def sb(shape, dt, tag, bufs=1):
            return pool.tile(shape, dt, name=tag, tag=tag, bufs=bufs, align_bytes=64)

        def f4k(shape, tag, bufs):
            return sb(shape, F32, tag, bufs)

        def b2k(shape):
            return sb(shape, BF16, "b2k", B2K)

        def bank(tag, bufs):
            return psum.tile([P, NB], F32, name=tag, tag=tag, bufs=bufs)

        half = sb([P, 1], F32, "half")
        ident = sb([P, P], F32, "ident")
        V.memset(half[:], 0.5)
        make_identity(nc, ident[:])

        wq = {n: (sb([P, KP, H], U32, "wq" + n), sb([P, KP, H], U8, "ws" + n)) for n in "hzr"}
        iq, isc = sb([P, KP, C], U32, "iq"), sb([P, KP, C], U8, "isc")
        dq, dsc = sb([P, KP, H], U32, "dq"), sb([P, KP, H], U8, "dsc")
        aq, asc = sb([P, TILES, KP * P], U32, "aq"), sb([P, TILES, KP * P], U8, "asc")
        bq, bsc = sb([P, TILES, KP * P], U32, "bq"), sb([P, TILES, KP * P], U8, "bsc")
        fq = [sb([P, TILES, P], U32, "fq%d" % n) for n in range(KP)]
        fsc = [sb([P, TILES, P], U8, "fsc%d" % n) for n in range(KP)]
        hg = [sb([P, PACK, H], BF16, "hg%d" % g) for g in range(KP)]
        ut = [sb([P, H], F32, "u%d" % i) for i in range(TILES)]

        az, ah, gg, raw, gr = {}, {}, {}, {}, {}
        qh, gm, ab, aT, gT, bT, dT = {}, {}, {}, {}, {}, {}, {}
        htp, nhp, e_ps, tr = {}, {}, {}, {}
        arh, hm, dn, d_ps, o_ps = {}, {}, {}, {}, {}

        def load_w(n, kp):
            raw[n, kp] = sb([P, PACK, H], BF16, "raw", 2)
            Q.dma_start(out=raw[n, kp][:], in_=w_h[n][:, kp])

        def load_in():
            raw["in"] = sb([P, KP, PACK, I], BF16, "raw", 2)
            Q.dma_start(out=raw["in"][:], in_=in_h)

        def load_az(i):
            az[i] = f4k([P, H], "az", AZB)
            Q.dma_start(out=az[i][:], in_=az_h[:, i // 4, i % 4, :])

        def load_ah(i):
            ah[i] = f4k([P, H], "ah", 3)
            Q.dma_start(out=ah[i][:], in_=ah_h[:, i // 4, i % 4, :])

        def load_g(i):
            gg[i] = sb([P, H], BF16, "gg", 3)
            Q.dma_start(out=gg[i][:], in_=g_h[:, i // 4, i % 4, :])

        def load_h(i):
            Q.dma_start(out=hg[i // 4][:, i % 4, :], in_=h_h[:, i // 4, i % 4, :])

        def load_ar(j):
            q, n = j % 4, j // 4
            g, t = q // 2, 2 * (q % 2)
            arh[j] = f4k([P, 2, NB], "ah", 3)
            Q.dma_start(out=arh[j][:], in_=ar_h[:, g, t:t + 2, n * NB:(n + 1) * NB])

        def cols(n):
            return slice(n * NB, (n + 1) * NB)

        def s_p(i):
            S.activation(out=ut[i][:], in_=az[i][:], func=ACT.Relu, bias=half[:], scale=-SIXTH)

        def s_qh(i):
            qh[i] = b2k([P, H])
            S.activation(out=qh[i][:], in_=ah[i][:], func=ACT.Square, scale=ROOT_1)

        def s_qz(i):
            gm[i] = b2k([P, H])
            S.activation(out=gm[i][:], in_=az[i][:], func=ACT.Square, scale=ROOT_3)

        def by_slot(x):
            return x.rearrange("p (k m t) -> p k m t", k=KP, t=PACK)

        def s_nh(i):
            nhp[i] = f4k([P, KP, PACK, P], "nh", 1)
            S.activation(out=nhp[i][:].rearrange("p k t m -> p k m t"), in_=by_slot(hg[i // 4][:, i % 4, :]), func=ACT.Copy, scale=-1.0)

        def words(key, src):
            tr[key] = psum.tile([P, KP * 2, P], F32, name="tr", tag="tr", bufs=2)
            w = src.bitcast(F32)
            for kp in range(KP):
                for u in range(2):
                    PE.transpose(tr[key][:, 2 * kp + u, :], w[:, 256 * kp + u:256 * (kp + 1):2], ident[:])

        def s_words(key):
            out = sb([P, KP, P, PACK], BF16, "T" + key[0], 1)
            S.copy(out=out[:].bitcast(F32), in_=tr[key][:].rearrange("p (k u) r -> p k r u", k=KP))
            return out

        def quant(codes, scales, src, fmt):
            V.quantize_mx(out=codes.bitcast(fmt), scales=scales, in_=src)

        def v_u(i):
            V.scalar_tensor_tensor(out=ut[i][:], in0=ut[i][:], scalar=1.0, in1=gg[i][:], op0=ALU.min, op1=ALU.mult)

        def v_A(i):
            a = b2k([P, H])
            V.scalar_tensor_tensor(out=a[:], in0=qh[i][:], scalar=EDGE, in1=ut[i][:], op0=ALU.is_lt, op1=ALU.mult)
            words(("a", i), a[:])

        def gz(eng, i, n):
            eng.tensor_tensor(out=ut[i][:, cols(n)], in0=gg[i][:, cols(n)], in1=ut[i][:, cols(n)], op=ALU.subtract)

        def v_qA(i):
            quant(aq[:, i], asc[:, i], aT[i][:].rearrange("p k r t -> p (k r t)"), E5M2X4)

        def v_mz(i):
            V.tensor_scalar(out=gm[i][:], in0=gm[i][:], scalar1=EDGE, scalar2=None, op0=ALU.is_lt)

        def v_gm(i):
            V.tensor_tensor(out=gm[i][:], in0=gm[i][:], in1=gg[i][:], op=ALU.mult)
            words(("g", i), gm[i][:])

        def v_ht(i):
            htp[i] = f4k([P, KP, PACK, P], "ht", 1)
            V.tensor_scalar(out=htp[i][:].rearrange("p k t m -> p k m t"), in0=by_slot(ah[i][:]), scalar1=-1.0, scalar2=1.0, op0=ALU.max, op1=ALU.min)
            for kp in range(KP):
                e_ps[i, kp] = bank("ed", 2)
                for t in range(PACK):
                    for src, first in ((htp, True), (nhp, False)):
                        PE.matmul(out=e_ps[i, kp][:, t * P:(t + 1) * P], lhsT=src[i][:, kp, t, :], rhs=ident[:], start=first, stop=not first, is_transpose=True)

        def v_B(i):
            bT[i] = sb([P, KP, P, PACK], BF16, "Tb", 1)
            for kp in range(KP):
                V.scalar_tensor_tensor(out=bT[i][:, kp], in0=e_ps[i, kp][:].rearrange("p (t r) -> p r t", t=PACK), scalar=-SIXTH, in1=gT[i][:, kp], op0=ALU.mult, op1=ALU.mult)

        def v_qB(i):
            quant(bq[:, i], bsc[:, i], bT[i][:].rearrange("p k r t -> p (k r t)"), E5M2X4)

        def s_r(j):
            hm[j] = b2k([P, 2, NB])
            S.activation(out=hm[j][:], in_=arh[j][:], func=ACT.Square, scale=ROOT_3)
            S.activation(out=arh[j][:], in_=arh[j][:], func=ACT.Relu, bias=half[:], scale=SIXTH)

        def v_hm(j):
            q, n = j % 4, j // 4
            g, t = q // 2, 2 * (q % 2)
            V.tensor_tensor(out=hm[j][:], in0=hm[j][:], in1=hg[g][:, t:t + 2, cols(n)], op=ALU.mult)

        def v_mr(j):
            V.tensor_scalar(out=hm[j][:], in0=hm[j][:], scalar1=EDGE, scalar2=None, op0=ALU.is_lt)

        def pe_d(j):
            q, n = j % 4, j // 4
            for s in range(2):
                i = 2 * q + s
                d_ps[j, s] = bank("ed", 2)
                for kp in range(KP):
                    PE.matmul_mx(
                        out=d_ps[j, s][:],
                        lhsT=aq[:, i, kp * P:(kp + 1) * P].bitcast(E5M2X4),
                        lhsT_scale=asc[:, i, kp * P:(kp + 1) * P],
                        rhs=wq["h"][0][:, kp, cols(n)].bitcast(E4M3X4),
                        rhs_scale=wq["h"][1][:, kp, cols(n)],
                        start=kp == 0, stop=kp == KP - 1,
                    )

        def v_ED(j):
            q, n = j % 4, j // 4
            g, t = q // 2, 2 * (q % 2)
            if t == 0:
                dn[g, n] = sb([P, PACK, NB], BF16, "dn", 2)
            for s in range(2):
                V.scalar_tensor_tensor(out=arh[j][:, s], in0=arh[j][:, s], scalar=1.0, in1=d_ps[j, s][:], op0=ALU.min, op1=ALU.mult)
                x = ut[2 * q + s][:, cols(n)]
                G.tensor_tensor(out=x, in0=arh[j][:, s], in1=x, op=ALU.add)
            key = ("d", j)
            tr[key] = psum.tile([P, KP * 2, P], F32, name="tr", tag="tr", bufs=2)
            for s in range(2):
                V.scalar_tensor_tensor(out=dn[g, n][:, t + s], in0=d_ps[j, s][:], scalar=SIXTH, in1=hm[j][:, s], op0=ALU.mult, op1=ALU.mult)
                w = dn[g, n][:, t + s].bitcast(F32)
                for u in range(2):
                    PE.transpose(tr[key][:, 2 * s + u, :], w[:, u:256:2], ident[:])

        def s_cD(j):
            dT[j] = s_words(("d", j))

        def v_qD(j):
            q, n = j % 4, j // 4
            quant(fq[n][:, 2 * q:2 * q + 2].rearrange("p i r -> p (i r)"), fsc[n][:, 2 * q:2 * q + 2].rearrange("p i r -> p (i r)"), dT[j][:].rearrange("p k r t -> p (k r t)"), E5M2X4)

        def pe_out0(i):
            for n in range(2):
                o_ps[i, n] = bank("oo", 4)
                for k in range(2 * KP):
                    kp = k % KP
                    if k < KP:
                        codes, scales = bq[:, i, kp * P:(kp + 1) * P], bsc[:, i, kp * P:(kp + 1) * P]
                    else:
                        codes, scales = fq[kp][:, i], fsc[kp][:, i]
                    wc, ws = wq["z" if k < KP else "r"]
                    PE.matmul_mx(
                        out=o_ps[i, n][:], lhsT=codes.bitcast(E5M2X4), lhsT_scale=scales,
                        rhs=wc[:, kp, cols(n)].bitcast(E4M3X4), rhs_scale=ws[:, kp, cols(n)],
                        start=k == 0, stop=k == 2 * KP - 1,
                    )

        def v_out(i):
            for n in range(2):
                x = ut[i][:, cols(n)]
                V.tensor_tensor(out=x, in0=o_ps[i, n][:], in1=x, op=ALU.add)
            Q.dma_start(out=o0_h[:, i // 4, i % 4, :], in_=ut[i][:])

        o1 = {}

        def out1(b, eng):
            m, n = b // 3, b % 3
            acc = bank("oo", 4)
            for g in range(KP):
                PE.matmul_mx(
                    out=acc[:],
                    lhsT=dq[:, g, m * P:(m + 1) * P].bitcast(E5M2X4), lhsT_scale=dsc[:, g, m * P:(m + 1) * P],
                    rhs=iq[:, g, cols(n)].bitcast(E4M3X4), rhs_scale=isc[:, g, cols(n)],
                    start=g == 0, stop=g == KP - 1,
                )
            if b % 2 == 0:
                o1[b // 2] = f4k([P, 2, NB], *(("az", AZB), ("nh", 1), ("az", AZB), ("ht", 1))[b // 2 % 4])
            dst = o1[b // 2][:, b % 2, :]
            if eng is S:
                S.copy(out=dst, in_=acc[:])
            else:
                V.tensor_copy(out=dst, in_=acc[:])
            Q.dma_start(out=out_1[m * P:(m + 1) * P, cols(n)], in_=dst)

        def new_gr(key):
            gr[key] = sb([P, H, PACK], BF16, "gr", 2)

        def il(eng, key, src, c0, c1, off=0):
            dst = gr[key][:, off + c0:off + c1, :].rearrange("p (c i) t -> p c t i", i=4)
            s = src[:, :, c0:c1].rearrange("p t (c i) -> p c t i", i=4)
            if eng is S:
                S.copy(out=dst, in_=s)
            else:
                V.tensor_copy(out=dst, in_=s)

        def q_cols(key, codes, scales, c0, c1, fmt):
            quant(codes, scales, gr[key][:, c0:c1, :].rearrange("p c t -> p (c t)"), fmt)

        def fill(eng, what):
            kind = what[0]
            if kind == "new":
                new_gr(what[1])
            elif kind == "il":
                key, c0, c1 = what[1:]
                if key in ("h0", "h1"):
                    src = hg[int(key[1])]
                elif key[0] == "d":
                    src = dn[key[1], key[2]]
                else:
                    src = raw[key]
                il(eng, key, src, c0, c1)
            elif kind == "ilin":
                g, c0, c1 = what[1:]
                il(eng, "in", raw["in"][:, g], c0, c1, g * I)
            elif kind == "qw":
                n, kp = what[1]
                c0, c1 = what[2:] if len(what) > 2 else (0, H)
                q_cols((n, kp), wq[n][0][:, kp, c0:c1], wq[n][1][:, kp, c0:c1], c0, c1, E4M3X4)
            elif kind == "qin":
                g = what[1]
                q_cols("in", iq[:, g, 0:I], isc[:, g, 0:I], g * I, (g + 1) * I, E4M3X4)
            elif kind == "qh":
                g, c0, c1 = what[1:]
                q_cols("h%d" % g, iq[:, g, I + c0:I + c1], isc[:, g, I + c0:I + c1], c0, c1, E4M3X4)
            elif kind == "qd":
                g, n, c0, c1 = what[1:]
                q_cols(("d", g, n), dq[:, g, n * NB + c0:n * NB + c1], dsc[:, g, n * NB + c0:n * NB + c1], c0, c1, E5M2X4)
            elif kind == "x":
                for b in range(what[1], what[2]):
                    out1(b, eng)
            elif kind == "out0":
                pe_out0(what[1])
            elif kind == "out":
                v_out(what[1])
            elif kind == "load":
                (load_in if what[1] == "in" else lambda: load_w(*what[1]))()

        def fills(eng, table, *key):
            for w in table.get(key, []):
                fill(eng, w)

        load_az(0)
        load_g(0)
        load_ah(0)
        load_h(0)
        load_w("h", 0)
        load_az(1)
        load_g(1)
        load_ah(1)
        load_h(1)
        s_p(0)
        s_qh(0)
        s_qz(0)
        s_nh(0)
        for k in range(TILES + 1):
            a = k if k < TILES else None
            m = k - 1 if k > 0 else None
            n = k + 1 if k + 1 < TILES else None
            if k + 2 < TILES:
                load_az(k + 2)
                load_g(k + 2)
                load_ah(k + 2)
                load_h(k + 2)
            fills(Q, LOADS, k)
            if a is not None:
                v_u(a)
                v_A(a)
                gz(G, a, 0)
            if n is not None:
                s_p(n)
                s_qh(n)
            if m is not None:
                v_B(m)
                v_qA(m)
            if a is not None:
                gz(V, a, 1)
                aT[a] = s_words(("a", a))
            if n is not None:
                s_qz(n)
            fills(S, S1, k, 0)
            if a is not None:
                v_mz(a)
                v_ht(a)
                v_gm(a)
            if m is not None:
                v_qB(m)
            if n is not None:
                s_nh(n)
            fills(S, S1, k, 1)
            fills(V, V1, k, 0)
            if a is not None:
                gT[a] = s_words(("g", a))
            fills(V, V1, k, 1)

        for j in range(9):
            if j + 2 < 8 and j > 0:
                load_ar(j + 2)
            fills(Q, LOADS, "u", j)
            if j == 0:
                for x in range(3):
                    load_ar(x)
                s_r(0)
                pe_d(0)
                v_mr(0)
                v_hm(0)
            if j < 8:
                v_ED(j)
            if j + 1 < 8:
                pe_d(j + 1)
                s_r(j + 1)
            fills(S, S2, j, 0)
            fills(V, V2, j, 0)
            if j > 0:
                v_qD(j - 1)
            if j < 8:
                s_cD(j)
            if j + 1 < 8:
                v_mr(j + 1)
            fills(V, V2, j, 1)
            if j + 1 < 8:
                v_hm(j + 1)
            fills(S, S2, j, 1)
            fills(V, V2, j, 2)
            fills(S, S2, j, 2)
